import numpy as np
import ml_dtypes


def mxq(x, axis, fmt="e4m3"):
    dtype, down = {"e4m3": (ml_dtypes.float8_e4m3fn, 7), "e5m2": (ml_dtypes.float8_e5m2, 14)}[fmt]
    v = np.moveaxis(np.asarray(x, np.float32).astype(ml_dtypes.bfloat16).astype(np.float64), axis, -1)
    blocks = v.reshape(v.shape[:-1] + (-1, 32))
    amax = np.abs(blocks).max(-1, keepdims=True)
    byte = np.maximum(np.where(amax > 0, np.frexp(amax)[1] - 1 + 127, 0) - down, 1)
    scale = np.exp2(byte - 127.0)
    codes = (blocks / scale).astype(np.float32).astype(dtype).astype(np.float64)
    return np.moveaxis((codes * scale).reshape(v.shape), -1, axis)


WIDE = False


def mx_kscale(k):
    if not WIDE:
        return np.ones(k)
    levels = np.array([10, -10, 5, -5, 0])
    a = np.random.permutation(np.resize(levels, k // 512 * 4)).reshape(k // 512, 4)
    idx = np.arange(k)
    return np.exp2(a[idx // 512, idx % 128 // 32])


BF16 = ml_dtypes.bfloat16


def bf(x):
    return np.asarray(x, np.float32).astype(BF16)


def f64(x):
    return np.asarray(x).astype(np.float64)


B, N_IN, N_OUT, D_IN, D_OUT = 2048, 4, 32, 1024, 16


def setup_inputs():
    s = mx_kscale(D_IN)
    inputs = np.random.standard_normal((B, N_IN, D_IN, 1)) * s[:, None]
    transform_mat = np.random.uniform(-1.0, 1.0, (1, N_IN, N_OUT, D_IN, D_OUT, 1)) * np.sqrt(3.0 / D_IN) / s[:, None, None]
    return {"inputs": bf(inputs), "transform_mat": bf(transform_mat)}


def reference(inputs, transform_mat):
    xq = mxq(f64(inputs)[..., 0], 2, "e4m3")
    wq = mxq(f64(transform_mat)[0, ..., 0], 2, "e4m3")
    prod = xq.transpose(1, 0, 2) @ wq.transpose(0, 2, 1, 3).reshape(N_IN, D_IN, N_OUT * D_OUT)
    votes = prod.reshape(N_IN, B, N_OUT, D_OUT).transpose(1, 0, 2, 3)
    return votes[..., None]

@@ -1,0 +1,177 @@
+from contextlib import ExitStack
+
+import concourse.mybir as mybir
+from concourse.masks import make_identity
+
+FLOPS = 2 * 2048 * 4 * 1024 * 512
+
+F32 = mybir.dt.float32
+BF16 = mybir.dt.bfloat16
+U32 = mybir.dt.uint32
+U8 = mybir.dt.uint8
+FP8X4 = mybir.dt.float8_e4m3fn_x4
+
+P = 128
+NT = 16
+NCAP = 4
+XBUFS = 8
+W_DVE_BANKS = (1,)
+
+
+def tile_transforming_t_kernel(tc, inputs, transform_mat, out):
+    nc = tc.nc
+    x_v = inputs.rearrange("(p j) n k x -> p j (n k x)", j=NT)
+    w_v = transform_mat.rearrange("a n m (h l) o x -> n (a m h) (l o x)", h=4)
+    out_v = out.rearrange("(p j) n m o x -> p j (n m o x)", j=NT)
+
+    with ExitStack() as ctx:
+        const = ctx.enter_context(tc.tile_pool(name="const", bufs=1))
+        wraw_pool = ctx.enter_context(tc.tile_pool(name="wraw", bufs=4))
+        wgrp_pool = ctx.enter_context(tc.tile_pool(name="wgrp", bufs=2))
+        xraw_pool = ctx.enter_context(tc.tile_pool(name="xraw", bufs=XBUFS))
+        xgrp_pool = ctx.enter_context(tc.tile_pool(name="xgrp", bufs=8))
+        xq_pool = ctx.enter_context(tc.tile_pool(name="xq", bufs=12))
+        out_pool = ctx.enter_context(tc.tile_pool(name="outp", bufs=6))
+        psum = ctx.enter_context(tc.psum_pool(name="psum", bufs=8))
+        ctx.enter_context(tc.manual_schedule())
+
+        ident = const.tile([P, P], F32, name="ident")
+        perm = const.tile([P, P], F32, name="perm")
+        w_codes = const.tile([P, NCAP, 1024], U32, name="w_codes", align_bytes=64)
+        w_scales = const.tile([P, NCAP, 1024], U8, name="w_scales", align_bytes=64)
+
+        w_raw = {}
+        x_raw = {}
+
+        def w_load(n):
+            t = wraw_pool.tile([P, 4096], BF16, name="w_raw")
+            nc.sync.dma_start(out=t[:], in_=w_v[n])
+            w_raw[n] = t
+
+        def x_load(j):
+            t = xraw_pool.tile([P, 4096], BF16, name="x_raw")
+            nc.sync.dma_start(out=t[:], in_=x_v[:, j, :])
+            x_raw[j] = t
+
+        w_load(0)
+        w_load(1)
+        x_load(0)
+        w_load(2)
+        w_load(3)
+        for j in range(1, XBUFS):
+            x_load(j)
+
+        make_identity(nc, ident[:])
+        nc.vector.tensor_copy(
+            out=perm[:].rearrange("p (u g m) -> p u g m", u=2, g=2),
+            in_=ident[:].rearrange("p (m g u) -> p u g m", g=2, u=2),
+        )
+
+        w_grp = {}
+
+        def w_prepare(n):
+            words = w_raw[n][:].bitcast(F32).rearrange("q (p c) -> q p c", c=16)
+            grp = wgrp_pool.tile([P, 4096], BF16, name="w_grp", align_bytes=64)
+            w_grp[n] = grp
+            grp_v = grp[:].rearrange("p (c o t) -> p c o t", o=16, t=4)
+            banks = []
+            for b2 in range(4):
+                bank = psum.tile([P, 512], F32, name="bank")
+                banks.append(bank)
+                bank_v = bank[:].rearrange("p (a u e c) -> p a e u c", a=2, u=2, e=2)
+                for a in range(2):
+                    for e in range(2):
+                        nc.tensor.transpose(bank_v[:, a, e], words[:, :, 8 * e + 2 * b2 + a], perm[:])
+            for b2 in range(4):
+                half = banks[b2][:].bitcast(BF16)
+                for a in range(2):
+                    o2 = 2 * b2 + a
+                    src = half[:, a * 512:(a + 1) * 512].rearrange("p (t c s) -> p c s t", t=4, s=2)
+                    dst = grp_v[:, :, 2 * o2:2 * o2 + 2, :]
+                    if b2 in W_DVE_BANKS:
+                        nc.vector.tensor_copy(out=dst, in_=src)
+                    else:
+                        nc.scalar.copy(out=dst, in_=src)
+
+        def w_quant(n):
+            nc.vector.quantize_mx(
+                out=w_codes[:, n, :].bitcast(FP8X4),
+                scales=w_scales[:, n, :],
+                in_=w_grp[n][:],
+            )
+
+        x_q = {}
+
+        def x_prepare(j):
+            words = x_raw[j][:].bitcast(F32)
+            banks = []
+            for n in range(NCAP):
+                bank = psum.tile([P, 512], F32, name="bank")
+                banks.append(bank)
+                for w in range(4):
+                    c0 = n * 512 + w * 128
+                    nc.tensor.transpose(bank[:, w * 128:(w + 1) * 128], words[:, c0:c0 + 128], ident[:])
+            if j + XBUFS < NT:
+                x_load(j + XBUFS)
+            grps = []
+
+            def cp(n, eng):
+                grp = xgrp_pool.tile([P, 1024], BF16, name="x_grp", align_bytes=64)
+                grps.append(grp)
+                dst = grp[:].bitcast(F32).rearrange("p (g b u) -> p g b u", g=2, u=2)
+                src = banks[n][:].rearrange("p (g u b) -> p g b u", g=2, u=2)
+                if eng == "v":
+                    nc.vector.tensor_copy(out=dst, in_=src)
+                else:
+                    nc.scalar.copy(out=dst, in_=src)
+
+            def qz(n):
+                codes = xq_pool.tile([P, 256], U32, name="x_codes", align_bytes=64)
+                scales = xq_pool.tile([P, 256], U8, name="x_scales", align_bytes=64)
+                nc.vector.quantize_mx(out=codes[:].bitcast(FP8X4), scales=scales[:], in_=grps[n][:])
+                x_q[(j, n)] = (codes, scales)
+
+            cp(0, "v")
+            cp(1, "v")
+            qz(0)
+            cp(2, "v")
+            cp(3, "s")
+            qz(1)
+            qz(2)
+            qz(3)
+
+        def x_multiply(j):
+            res = out_pool.tile([P, 2048], F32, name="res")
+            accs = []
+            for n in range(NCAP):
+                acc = psum.tile([P, 512], F32, name="bank")
+                accs.append(acc)
+                codes, scales = x_q[(j, n)]
+                for g in range(2):
+                    nc.tensor.matmul_mx(
+                        out=acc[:],
+                        lhsT=codes[:, g * 128:(g + 1) * 128].bitcast(FP8X4),
+                        lhsT_scale=scales[:, g * 128:(g + 1) * 128],
+                        rhs=w_codes[:, n, g * 512:(g + 1) * 512].bitcast(FP8X4),
+                        rhs_scale=w_scales[:, n, g * 512:(g + 1) * 512],
+                        start=(g == 0),
+                        stop=(g == 1),
+                    )
+            for n in range(NCAP):
+                nc.scalar.copy(out=res[:, n * 512:(n + 1) * 512], in_=accs[n][:])
+            nc.sync.dma_start(out=out_v[:, j, :], in_=res[:])
+
+        w_prepare(0)
+        w_prepare(1)
+        w_quant(0)
+        x_prepare(0)
+        w_quant(1)
+        w_prepare(2)
+        w_prepare(3)
+        w_quant(2)
+        x_prepare(1)
+        w_quant(3)
+        for j in range(NT):
+            if j + 2 < NT:
+                x_prepare(j + 2)
+            x_multiply(j)

@@ -14,8 +14,7 @@ FP8X4 = mybir.dt.float8_e4m3fn_x4
 P = 128
 NT = 16
 NCAP = 4
-XBUFS = 8
-W_DVE_BANKS = (1,)
+W_DVE_BANKS = ((1, 3), (1,), (1, 3), (1,))
 
 
 def tile_transforming_t_kernel(tc, inputs, transform_mat, out):
@@ -28,10 +27,10 @@ def tile_transforming_t_kernel(tc, inputs, transform_mat, out):
         const = ctx.enter_context(tc.tile_pool(name="const", bufs=1))
         wraw_pool = ctx.enter_context(tc.tile_pool(name="wraw", bufs=4))
         wgrp_pool = ctx.enter_context(tc.tile_pool(name="wgrp", bufs=2))
-        xraw_pool = ctx.enter_context(tc.tile_pool(name="xraw", bufs=XBUFS))
+        xraw_pool = ctx.enter_context(tc.tile_pool(name="xraw", bufs=4))
         xgrp_pool = ctx.enter_context(tc.tile_pool(name="xgrp", bufs=8))
         xq_pool = ctx.enter_context(tc.tile_pool(name="xq", bufs=12))
-        out_pool = ctx.enter_context(tc.tile_pool(name="outp", bufs=6))
+        out_pool = ctx.enter_context(tc.tile_pool(name="outp", bufs=4))
         psum = ctx.enter_context(tc.psum_pool(name="psum", bufs=8))
         ctx.enter_context(tc.manual_schedule())
 
@@ -48,18 +47,21 @@ def tile_transforming_t_kernel(tc, inputs, transform_mat, out):
             nc.sync.dma_start(out=t[:], in_=w_v[n])
             w_raw[n] = t
 
-        def x_load(j):
-            t = xraw_pool.tile([P, 4096], BF16, name="x_raw")
-            nc.sync.dma_start(out=t[:], in_=x_v[:, j, :])
-            x_raw[j] = t
+        def x_load_pair(g):
+            t = xraw_pool.tile([P, 2, 4096], BF16, name="x_raw")
+            nc.sync.dma_start(out=t[:], in_=x_v[:, 2 * g:2 * g + 2, :])
+            x_raw[g] = t
 
+        first = xraw_pool.tile([P, 2, 4096], BF16, name="x_raw")
+        x_raw[0] = first
         w_load(0)
         w_load(1)
-        x_load(0)
+        nc.sync.dma_start(out=first[:, 0, :], in_=x_v[:, 0, :])
         w_load(2)
         w_load(3)
-        for j in range(1, XBUFS):
-            x_load(j)
+        nc.sync.dma_start(out=first[:, 1, :], in_=x_v[:, 1, :])
+        for g in range(1, 4):
+            x_load_pair(g)
 
         make_identity(nc, ident[:])
         nc.vector.tensor_copy(
@@ -88,7 +90,7 @@ def tile_transforming_t_kernel(tc, inputs, transform_mat, out):
                     o2 = 2 * b2 + a
                     src = half[:, a * 512:(a + 1) * 512].rearrange("p (t c s) -> p c s t", t=4, s=2)
                     dst = grp_v[:, :, 2 * o2:2 * o2 + 2, :]
-                    if b2 in W_DVE_BANKS:
+                    if b2 in W_DVE_BANKS[n]:
                         nc.vector.tensor_copy(out=dst, in_=src)
                     else:
                         nc.scalar.copy(out=dst, in_=src)
@@ -103,7 +105,7 @@ def tile_transforming_t_kernel(tc, inputs, transform_mat, out):
         x_q = {}
 
         def x_prepare(j):
-            words = x_raw[j][:].bitcast(F32)
+            words = x_raw[j // 2][:, j % 2, :].bitcast(F32)
             banks = []
             for n in range(NCAP):
                 bank = psum.tile([P, 512], F32, name="bank")
@@ -111,8 +113,8 @@ def tile_transforming_t_kernel(tc, inputs, transform_mat, out):
                 for w in range(4):
                     c0 = n * 512 + w * 128
                     nc.tensor.transpose(bank[:, w * 128:(w + 1) * 128], words[:, c0:c0 + 128], ident[:])
-            if j + XBUFS < NT:
-                x_load(j + XBUFS)
+            if j % 2 == 1 and j // 2 + 4 < NT // 2:
+                x_load_pair(j // 2 + 4)
             grps = []
 
             def cp(n, eng):
@@ -134,14 +136,18 @@ def tile_transforming_t_kernel(tc, inputs, transform_mat, out):
             cp(0, "v")
             cp(1, "v")
             qz(0)
-            cp(2, "v")
+            cp(2, "s" if j < 2 else "v")
             cp(3, "s")
             qz(1)
             qz(2)
             qz(3)
 
+        res_of = {}
+
         def x_multiply(j):
-            res = out_pool.tile([P, 2048], F32, name="res")
+            if j % 2 == 0:
+                res_of[j // 2] = out_pool.tile([P, 2, 2048], F32, name="res")
+            res = res_of[j // 2]
             accs = []
             for n in range(NCAP):
                 acc = psum.tile([P, 512], F32, name="bank")
@@ -158,8 +164,11 @@ def tile_transforming_t_kernel(tc, inputs, transform_mat, out):
                         stop=(g == 1),
                     )
             for n in range(NCAP):
-                nc.scalar.copy(out=res[:, n * 512:(n + 1) * 512], in_=accs[n][:])
-            nc.sync.dma_start(out=out_v[:, j, :], in_=res[:])
+                nc.scalar.copy(out=res[:, j % 2, n * 512:(n + 1) * 512], in_=accs[n][:])
+            if j >= NT - 2:
+                nc.sync.dma_start(out=out_v[:, j, :], in_=res[:, j % 2, :])
+            elif j % 2 == 1:
+                nc.sync.dma_start(out=out_v[:, j - 1:j + 1, :], in_=res[:])
 
         w_prepare(0)
         w_prepare(1)
@@ -169,9 +178,9 @@ def tile_transforming_t_kernel(tc, inputs, transform_mat, out):
         w_prepare(2)
         w_prepare(3)
         w_quant(2)
-        x_prepare(1)
         w_quant(3)
+        x_prepare(1)
         for j in range(NT):
-            if j + 2 < NT:
-                x_prepare(j + 2)
+            if 1 <= j < NT - 1:
+                x_prepare(j + 1)
             x_multiply(j)

@@ -164,10 +164,16 @@ def tile_transforming_t_kernel(tc, inputs, transform_mat, out):
                         stop=(g == 1),
                     )
             for n in range(NCAP):
-                nc.scalar.copy(out=res[:, j % 2, n * 512:(n + 1) * 512], in_=accs[n][:])
-            if j >= NT - 2:
+                cols = slice(n * 512, (n + 1) * 512)
+                if j == NT - 1 and n % 2 == 1:
+                    nc.vector.tensor_copy(out=res[:, j % 2, cols], in_=accs[n][:])
+                else:
+                    nc.scalar.copy(out=res[:, j % 2, cols], in_=accs[n][:])
+                if j == NT - 1:
+                    nc.sync.dma_start(out=out_v[:, j, cols], in_=res[:, j % 2, cols])
+            if j == NT - 2:
                 nc.sync.dma_start(out=out_v[:, j, :], in_=res[:, j % 2, :])
-            elif j % 2 == 1:
+            elif j % 2 == 1 and j < NT - 2:
                 nc.sync.dma_start(out=out_v[:, j - 1:j + 1, :], in_=res[:])
 
         w_prepare(0)

@@ -169,11 +169,9 @@ def tile_transforming_t_kernel(tc, inputs, transform_mat, out):
                     nc.vector.tensor_copy(out=res[:, j % 2, cols], in_=accs[n][:])
                 else:
                     nc.scalar.copy(out=res[:, j % 2, cols], in_=accs[n][:])
-                if j == NT - 1:
-                    nc.sync.dma_start(out=out_v[:, j, cols], in_=res[:, j % 2, cols])
-            if j == NT - 2:
+            if j >= NT - 4:
                 nc.sync.dma_start(out=out_v[:, j, :], in_=res[:, j % 2, :])
-            elif j % 2 == 1 and j < NT - 2:
+            elif j % 2 == 1:
                 nc.sync.dma_start(out=out_v[:, j - 1:j + 1, :], in_=res[:])
 
         w_prepare(0)

@@ -25,12 +25,10 @@ def tile_transforming_t_kernel(tc, inputs, transform_mat, out):
 
     with ExitStack() as ctx:
         const = ctx.enter_context(tc.tile_pool(name="const", bufs=1))
-        wraw_pool = ctx.enter_context(tc.tile_pool(name="wraw", bufs=4))
+        big_pool = ctx.enter_context(tc.tile_pool(name="big", bufs=5))
         wgrp_pool = ctx.enter_context(tc.tile_pool(name="wgrp", bufs=2))
-        xraw_pool = ctx.enter_context(tc.tile_pool(name="xraw", bufs=4))
         xgrp_pool = ctx.enter_context(tc.tile_pool(name="xgrp", bufs=8))
         xq_pool = ctx.enter_context(tc.tile_pool(name="xq", bufs=12))
-        out_pool = ctx.enter_context(tc.tile_pool(name="outp", bufs=4))
         psum = ctx.enter_context(tc.psum_pool(name="psum", bufs=8))
         ctx.enter_context(tc.manual_schedule())
 
@@ -39,29 +37,28 @@ def tile_transforming_t_kernel(tc, inputs, transform_mat, out):
         w_codes = const.tile([P, NCAP, 1024], U32, name="w_codes", align_bytes=64)
         w_scales = const.tile([P, NCAP, 1024], U8, name="w_scales", align_bytes=64)
 
-        w_raw = {}
-        x_raw = {}
+        w_all = big_pool.tile([P, NCAP, 4096], BF16, name="big")
+        x_quad = []
+        for q in range(4):
+            xq4 = big_pool.tile([P, 4, 4096], BF16, name="big")
+            x_quad.append(xq4)
 
         def w_load(n):
-            t = wraw_pool.tile([P, 4096], BF16, name="w_raw")
-            nc.sync.dma_start(out=t[:], in_=w_v[n])
-            w_raw[n] = t
+            nc.sync.dma_start(out=w_all[:, n, :], in_=w_v[n])
 
-        def x_load_pair(g):
-            t = xraw_pool.tile([P, 2, 4096], BF16, name="x_raw")
-            nc.sync.dma_start(out=t[:], in_=x_v[:, 2 * g:2 * g + 2, :])
-            x_raw[g] = t
+        def x_load(j0, j1):
+            nc.sync.dma_start(out=x_quad[j0 // 4][:, j0 % 4:(j1 - 1) % 4 + 1, :], in_=x_v[:, j0:j1, :])
 
-        first = xraw_pool.tile([P, 2, 4096], BF16, name="x_raw")
-        x_raw[0] = first
         w_load(0)
         w_load(1)
-        nc.sync.dma_start(out=first[:, 0, :], in_=x_v[:, 0, :])
+        x_load(0, 1)
         w_load(2)
         w_load(3)
-        nc.sync.dma_start(out=first[:, 1, :], in_=x_v[:, 1, :])
-        for g in range(1, 4):
-            x_load_pair(g)
+        x_load(1, 2)
+        x_load(2, 4)
+        x_load(4, 8)
+        x_load(8, 12)
+        x_load(12, 16)
 
         make_identity(nc, ident[:])
         nc.vector.tensor_copy(
@@ -72,7 +69,7 @@ def tile_transforming_t_kernel(tc, inputs, transform_mat, out):
         w_grp = {}
 
         def w_prepare(n):
-            words = w_raw[n][:].bitcast(F32).rearrange("q (p c) -> q p c", c=16)
+            words = w_all[:, n, :].bitcast(F32).rearrange("q (p c) -> q p c", c=16)
             grp = wgrp_pool.tile([P, 4096], BF16, name="w_grp", align_bytes=64)
             w_grp[n] = grp
             grp_v = grp[:].rearrange("p (c o t) -> p c o t", o=16, t=4)
@@ -105,7 +102,7 @@ def tile_transforming_t_kernel(tc, inputs, transform_mat, out):
         x_q = {}
 
         def x_prepare(j):
-            words = x_raw[j // 2][:, j % 2, :].bitcast(F32)
+            words = x_quad[j // 4][:, j % 4, :].bitcast(F32)
             banks = []
             for n in range(NCAP):
                 bank = psum.tile([P, 512], F32, name="bank")
@@ -113,8 +110,6 @@ def tile_transforming_t_kernel(tc, inputs, transform_mat, out):
                 for w in range(4):
                     c0 = n * 512 + w * 128
                     nc.tensor.transpose(bank[:, w * 128:(w + 1) * 128], words[:, c0:c0 + 128], ident[:])
-            if j % 2 == 1 and j // 2 + 4 < NT // 2:
-                x_load_pair(j // 2 + 4)
             grps = []
 
             def cp(n, eng):
@@ -145,9 +140,9 @@ def tile_transforming_t_kernel(tc, inputs, transform_mat, out):
         res_of = {}
 
         def x_multiply(j):
-            if j % 2 == 0:
-                res_of[j // 2] = out_pool.tile([P, 2, 2048], F32, name="res")
-            res = res_of[j // 2]
+            if j % 4 == 0:
+                res_of[j // 4] = big_pool.tile([P, 4, 2048], F32, name="big")
+            res = res_of[j // 4]
             accs = []
             for n in range(NCAP):
                 acc = psum.tile([P, 512], F32, name="bank")
@@ -166,13 +161,13 @@ def tile_transforming_t_kernel(tc, inputs, transform_mat, out):
             for n in range(NCAP):
                 cols = slice(n * 512, (n + 1) * 512)
                 if j == NT - 1 and n % 2 == 1:
-                    nc.vector.tensor_copy(out=res[:, j % 2, cols], in_=accs[n][:])
+                    nc.vector.tensor_copy(out=res[:, j % 4, cols], in_=accs[n][:])
                 else:
-                    nc.scalar.copy(out=res[:, j % 2, cols], in_=accs[n][:])
+                    nc.scalar.copy(out=res[:, j % 4, cols], in_=accs[n][:])
             if j >= NT - 4:
-                nc.sync.dma_start(out=out_v[:, j, :], in_=res[:, j % 2, :])
+                nc.sync.dma_start(out=out_v[:, j, :], in_=res[:, j % 4, :])
             elif j % 2 == 1:
-                nc.sync.dma_start(out=out_v[:, j - 1:j + 1, :], in_=res[:])
+                nc.sync.dma_start(out=out_v[:, j - 1:j + 1, :], in_=res[:, j % 4 - 1:j % 4 + 1, :])
 
         w_prepare(0)
         w_prepare(1)

@@ -19,9 +19,9 @@ W_DVE_BANKS = ((1, 3), (1,), (1, 3), (1,))
 
 def tile_transforming_t_kernel(tc, inputs, transform_mat, out):
     nc = tc.nc
-    x_v = inputs.rearrange("(p j) n k x -> p j (n k x)", j=NT)
+    x_v = inputs.rearrange("(q p j) n k x -> q p j (n k x)", q=4, j=4)
     w_v = transform_mat.rearrange("a n m (h l) o x -> n (a m h) (l o x)", h=4)
-    out_v = out.rearrange("(p j) n m o x -> p j (n m o x)", j=NT)
+    out_v = out.rearrange("(q p j) n m o x -> q p j (n m o x)", q=4, j=4)
 
     with ExitStack() as ctx:
         const = ctx.enter_context(tc.tile_pool(name="const", bufs=1))
@@ -47,7 +47,7 @@ def tile_transforming_t_kernel(tc, inputs, transform_mat, out):
             nc.sync.dma_start(out=w_all[:, n, :], in_=w_v[n])
 
         def x_load(j0, j1):
-            nc.sync.dma_start(out=x_quad[j0 // 4][:, j0 % 4:(j1 - 1) % 4 + 1, :], in_=x_v[:, j0:j1, :])
+            nc.sync.dma_start(out=x_quad[j0 // 4][:, j0 % 4:(j1 - 1) % 4 + 1, :], in_=x_v[j0 // 4][:, j0 % 4:(j1 - 1) % 4 + 1, :])
 
         w_load(0)
         w_load(1)
@@ -165,9 +165,9 @@ def tile_transforming_t_kernel(tc, inputs, transform_mat, out):
                 else:
                     nc.scalar.copy(out=res[:, j % 4, cols], in_=accs[n][:])
             if j >= NT - 4:
-                nc.sync.dma_start(out=out_v[:, j, :], in_=res[:, j % 4, :])
+                nc.sync.dma_start(out=out_v[j // 4][:, j % 4, :], in_=res[:, j % 4, :])
             elif j % 2 == 1:
-                nc.sync.dma_start(out=out_v[:, j - 1:j + 1, :], in_=res[:, j % 4 - 1:j % 4 + 1, :])
+                nc.sync.dma_start(out=out_v[j // 4][:, j % 4 - 1:j % 4 + 1, :], in_=res[:, j % 4 - 1:j % 4 + 1, :])
 
         w_prepare(0)
         w_prepare(1)

from contextlib import ExitStack

import concourse.mybir as mybir
from concourse.masks import make_identity

FLOPS = 2 * 2048 * 4 * 1024 * 512

F32 = mybir.dt.float32
BF16 = mybir.dt.bfloat16
U32 = mybir.dt.uint32
U8 = mybir.dt.uint8
FP8X4 = mybir.dt.float8_e4m3fn_x4

P = 128
NT = 16
NCAP = 4
W_DVE_BANKS = ((1, 3), (1,), (1, 3), (1,))


def tile_transforming_t_kernel(tc, inputs, transform_mat, out):
    nc = tc.nc
    x_v = inputs.rearrange("(q p j) n k x -> q p j (n k x)", q=4, j=4)
    w_v = transform_mat.rearrange("a n m (h l) o x -> n (a m h) (l o x)", h=4)
    out_v = out.rearrange("(q p j) n m o x -> q p j (n m o x)", q=4, j=4)

    with ExitStack() as ctx:
        const = ctx.enter_context(tc.tile_pool(name="const", bufs=1))
        big_pool = ctx.enter_context(tc.tile_pool(name="big", bufs=5))
        wgrp_pool = ctx.enter_context(tc.tile_pool(name="wgrp", bufs=2))
        xgrp_pool = ctx.enter_context(tc.tile_pool(name="xgrp", bufs=8))
        xq_pool = ctx.enter_context(tc.tile_pool(name="xq", bufs=12))
        psum = ctx.enter_context(tc.psum_pool(name="psum", bufs=8))
        ctx.enter_context(tc.manual_schedule())

        ident = const.tile([P, P], F32, name="ident")
        perm = const.tile([P, P], F32, name="perm")
        w_codes = const.tile([P, NCAP, 1024], U32, name="w_codes", align_bytes=64)
        w_scales = const.tile([P, NCAP, 1024], U8, name="w_scales", align_bytes=64)

        w_all = big_pool.tile([P, NCAP, 4096], BF16, name="big")
        x_quad = []
        for q in range(4):
            xq4 = big_pool.tile([P, 4, 4096], BF16, name="big")
            x_quad.append(xq4)

        def w_load(n):
            nc.sync.dma_start(out=w_all[:, n, :], in_=w_v[n])

        def x_load(j0, j1):
            nc.sync.dma_start(out=x_quad[j0 // 4][:, j0 % 4:(j1 - 1) % 4 + 1, :], in_=x_v[j0 // 4][:, j0 % 4:(j1 - 1) % 4 + 1, :])

        w_load(0)
        w_load(1)
        x_load(0, 1)
        w_load(2)
        w_load(3)
        x_load(1, 2)
        x_load(2, 4)
        x_load(4, 8)
        x_load(8, 12)
        x_load(12, 16)

        make_identity(nc, ident[:])
        nc.vector.tensor_copy(
            out=perm[:].rearrange("p (u g m) -> p u g m", u=2, g=2),
            in_=ident[:].rearrange("p (m g u) -> p u g m", g=2, u=2),
        )

        w_grp = {}

        def w_prepare(n):
            words = w_all[:, n, :].bitcast(F32).rearrange("q (p c) -> q p c", c=16)
            grp = wgrp_pool.tile([P, 4096], BF16, name="w_grp", align_bytes=64)
            w_grp[n] = grp
            grp_v = grp[:].rearrange("p (c o t) -> p c o t", o=16, t=4)
            banks = []
            for b2 in range(4):
                bank = psum.tile([P, 512], F32, name="bank")
                banks.append(bank)
                bank_v = bank[:].rearrange("p (a u e c) -> p a e u c", a=2, u=2, e=2)
                for a in range(2):
                    for e in range(2):
                        nc.tensor.transpose(bank_v[:, a, e], words[:, :, 8 * e + 2 * b2 + a], perm[:])
            for b2 in range(4):
                half = banks[b2][:].bitcast(BF16)
                for a in range(2):
                    o2 = 2 * b2 + a
                    src = half[:, a * 512:(a + 1) * 512].rearrange("p (t c s) -> p c s t", t=4, s=2)
                    dst = grp_v[:, :, 2 * o2:2 * o2 + 2, :]
                    if b2 in W_DVE_BANKS[n]:
                        nc.vector.tensor_copy(out=dst, in_=src)
                    else:
                        nc.scalar.copy(out=dst, in_=src)

        def w_quant(n):
            nc.vector.quantize_mx(
                out=w_codes[:, n, :].bitcast(FP8X4),
                scales=w_scales[:, n, :],
                in_=w_grp[n][:],
            )

        x_q = {}

        def x_prepare(j):
            words = x_quad[j // 4][:, j % 4, :].bitcast(F32)
            banks = []
            for n in range(NCAP):
                bank = psum.tile([P, 512], F32, name="bank")
                banks.append(bank)
                for w in range(4):
                    c0 = n * 512 + w * 128
                    nc.tensor.transpose(bank[:, w * 128:(w + 1) * 128], words[:, c0:c0 + 128], ident[:])
            grps = []

            def cp(n, eng):
                grp = xgrp_pool.tile([P, 1024], BF16, name="x_grp", align_bytes=64)
                grps.append(grp)
                dst = grp[:].bitcast(F32).rearrange("p (g b u) -> p g b u", g=2, u=2)
                src = banks[n][:].rearrange("p (g u b) -> p g b u", g=2, u=2)
                if eng == "v":
                    nc.vector.tensor_copy(out=dst, in_=src)
                else:
                    nc.scalar.copy(out=dst, in_=src)

            def qz(n):
                codes = xq_pool.tile([P, 256], U32, name="x_codes", align_bytes=64)
                scales = xq_pool.tile([P, 256], U8, name="x_scales", align_bytes=64)
                nc.vector.quantize_mx(out=codes[:].bitcast(FP8X4), scales=scales[:], in_=grps[n][:])
                x_q[(j, n)] = (codes, scales)

            cp(0, "v")
            cp(1, "v")
            qz(0)
            cp(2, "s" if j < 2 else "v")
            cp(3, "s")
            qz(1)
            qz(2)
            qz(3)

        res_of = {}

        def x_multiply(j):
            if j % 4 == 0:
                res_of[j // 4] = big_pool.tile([P, 4, 2048], F32, name="big")
            res = res_of[j // 4]
            accs = []
            for n in range(NCAP):
                acc = psum.tile([P, 512], F32, name="bank")
                accs.append(acc)
                codes, scales = x_q[(j, n)]
                for g in range(2):
                    nc.tensor.matmul_mx(
                        out=acc[:],
                        lhsT=codes[:, g * 128:(g + 1) * 128].bitcast(FP8X4),
                        lhsT_scale=scales[:, g * 128:(g + 1) * 128],
                        rhs=w_codes[:, n, g * 512:(g + 1) * 512].bitcast(FP8X4),
                        rhs_scale=w_scales[:, n, g * 512:(g + 1) * 512],
                        start=(g == 0),
                        stop=(g == 1),
                    )
            for n in range(NCAP):
                cols = slice(n * 512, (n + 1) * 512)
                if j == NT - 1 and n % 2 == 1:
                    nc.vector.tensor_copy(out=res[:, j % 4, cols], in_=accs[n][:])
                else:
                    nc.scalar.copy(out=res[:, j % 4, cols], in_=accs[n][:])
            if j >= NT - 4:
                nc.sync.dma_start(out=out_v[j // 4][:, j % 4, :], in_=res[:, j % 4, :])
            elif j % 2 == 1:
                nc.sync.dma_start(out=out_v[j // 4][:, j % 4 - 1:j % 4 + 1, :], in_=res[:, j % 4 - 1:j % 4 + 1, :])

        w_prepare(0)
        w_prepare(1)
        w_quant(0)
        x_prepare(0)
        w_quant(1)
        w_prepare(2)
        w_prepare(3)
        w_quant(2)
        w_quant(3)
        x_prepare(1)
        for j in range(NT):
            if 1 <= j < NT - 1:
                x_prepare(j + 1)
            x_multiply(j)
